import numpy as np
import ml_dtypes


def mxq(x, axis, fmt="e4m3"):
    dtype, down = {"e4m3": (ml_dtypes.float8_e4m3fn, 7), "e5m2": (ml_dtypes.float8_e5m2, 14)}[fmt]
    v = np.moveaxis(np.asarray(x, np.float32).astype(ml_dtypes.bfloat16).astype(np.float64), axis, -1)
    blocks = v.reshape(v.shape[:-1] + (-1, 32))
    amax = np.abs(blocks).max(-1, keepdims=True)
    byte = np.maximum(np.where(amax > 0, np.frexp(amax)[1] - 1 + 127, 0) - down, 1)
    scale = np.exp2(byte - 127.0)
    codes = (blocks / scale).astype(np.float32).astype(dtype).astype(np.float64)
    return np.moveaxis((codes * scale).reshape(v.shape), -1, axis)


WIDE = False


def mx_kscale(k):
    if not WIDE:
        return np.ones(k)
    levels = np.array([10, -10, 5, -5, 0])
    if k % 512:
        return np.exp2(np.random.permutation(np.resize(levels, k // 32))).repeat(32)
    a = np.empty((k // 512, 16))
    for p in range(k // 512):
        a[p, :8] = np.random.permutation(np.resize(levels, 8))
        for g in range(8):
            far = levels[np.abs(levels - a[p, g]) >= 10]
            a[p, g + 8] = far[np.random.randint(len(far))]
    return np.exp2(a.ravel()).repeat(32)


BF16 = ml_dtypes.bfloat16


def bf(x):
    return np.asarray(x, np.float32).astype(BF16)


def f64(x):
    return np.asarray(x).astype(np.float64)


E, F, H, MID, OUT = 16384, 64, 192, 512, 128
D = 2 * (F + H)
IN = D + 1


def setup_inputs():
    s = mx_kscale(D)
    t = mx_kscale(MID)
    w1 = np.concatenate([np.random.standard_normal((MID, D)) / np.sqrt(D) / s[None, :],
                         np.random.standard_normal((MID, 1)) * 0.5], axis=1) * t[:, None]
    return {"dst_node_feat": bf(np.random.standard_normal((E, F)) * s[:F]),
            "dst_node_hidden": bf(np.random.standard_normal((E, H)) * s[F:F + H]),
            "src_node_feat": bf(np.random.standard_normal((E, F)) * s[F + H:2 * F + H]),
            "src_node_hidden": bf(np.random.standard_normal((E, H)) * s[2 * F + H:]),
            "edge_feat": bf(np.random.standard_normal(E)),
            "W1": bf(w1),
            "b1": bf(np.random.standard_normal(MID) * 0.3 * t),
            "W2": bf(np.random.standard_normal((OUT, MID)) / np.sqrt(MID) / t[None, :]),
            "b2": bf(np.random.standard_normal(OUT) * 0.3)}


def reference(dst_node_feat, dst_node_hidden, src_node_feat, src_node_hidden, edge_feat, W1, b1, W2, b2):
    x = np.concatenate([f64(dst_node_feat), f64(dst_node_hidden), f64(src_node_feat), f64(src_node_hidden),
                        f64(edge_feat)[:, None]], axis=1)
    w1 = f64(W1)
    pre = (mxq(x[:, :D], 1, "e4m3") @ mxq(w1[:, :D], 1, "e4m3").T) + x[:, D:] * w1[:, D] + f64(b1)
    h = np.maximum(pre, 0.0)
    return np.tanh((mxq(h, 1, "e4m3") @ mxq(f64(W2), 1, "e4m3").T) + f64(b2))

@@ -1,0 +1,311 @@
+from contextlib import ExitStack
+
+import concourse.mybir as mybir
+from concourse.masks import make_identity
+
+E, F, H, MID, OUT = 16384, 64, 192, 512, 128
+D = 2 * (F + H)
+FLOPS = 2 * E * MID * (D + 1) + 2 * E * MID * OUT
+
+F32 = mybir.dt.float32
+BF16 = mybir.dt.bfloat16
+U32 = mybir.dt.uint32
+U8 = mybir.dt.uint8
+FP8X4 = mybir.dt.float8_e4m3fn_x4
+ALU = mybir.AluOpType
+ACT = mybir.ActivationFunctionType
+
+BANK_DT = F32
+
+P = 128
+TILES = 4
+GROUP = TILES * P
+CHUNK_TILES = 8
+CHUNK = CHUNK_TILES * P
+NG = E // GROUP
+NCH = E // CHUNK
+
+
+def tile_edgenetwork_kernel(
+    tc, dst_node_feat, dst_node_hidden, src_node_feat, src_node_hidden, edge_feat, W1, b1, W2, b2, out
+):
+    nc = tc.nc
+    parts = (
+        (dst_node_feat, 0, F),
+        (dst_node_hidden, F, H),
+        (src_node_feat, F + H, F),
+        (src_node_hidden, 2 * F + H, H),
+    )
+
+    with ExitStack() as ctx:
+        const = ctx.enter_context(tc.tile_pool(name="const", bufs=1))
+        work = ctx.enter_context(tc.tile_pool(name="work", bufs=2))
+        psum = ctx.enter_context(tc.psum_pool(name="psum", bufs=1))
+        ctx.enter_context(tc.manual_schedule())
+
+        xs_of = {}
+        xt_of = {}
+        xg_of = {}
+        xq_of = {}
+        ef_of = {}
+        c_of = {}
+        s1_of = {}
+        hp_of = {}
+        hq_of = {}
+        hc_of = {}
+        s2_of = {}
+        yt_of = {}
+        s3_of = {}
+        y_of = {}
+
+        def load(ch, pieces):
+            xs = work.tile([P, CHUNK_TILES, D], BF16, name="xs", tag="xs", bufs=3)
+            xs_of[ch] = xs
+            rows = slice(ch * CHUNK, (ch + 1) * CHUNK)
+            step = CHUNK_TILES // pieces
+            for j0 in range(0, CHUNK_TILES, step):
+                for src, k0, width in parts:
+                    nc.sync.dma_start(
+                        out=xs[:, j0 : j0 + step, k0 : k0 + width],
+                        in_=src[rows, :].rearrange("(p j) k -> p j k", j=CHUNK_TILES)[:, j0 : j0 + step, :],
+                    )
+
+        warm = const.tile([P, 1], F32, name="warm", tag="warm")
+        nc.vector.memset(warm[:], 0.0)
+        warm2 = const.tile([P, 1], F32, name="warm2", tag="warm2")
+        nc.scalar.activation(out=warm2[:], in_=warm[:], func=ACT.Tanh)
+
+        ident_b = const.tile([P, P], BF16, name="ident_b", tag="ident_b")
+        make_identity(nc, ident_b[:])
+        ident_f = const.tile([P, P], F32, name="ident_f", tag="ident_f")
+        make_identity(nc, ident_f[:])
+
+        ef4 = const.tile([P, CHUNK], BF16, name="ef4", tag="ef4")
+        nc.vector.memset(ef4[:], 0.0)
+        nc.sync.dma_start(out=ef4[0:NCH, :], in_=edge_feat.rearrange("(c r) -> c r", r=CHUNK))
+        wslab = const.tile([P, TILES, 16], BF16, name="wslab", tag="wslab")
+        nc.sync.dma_start(out=wslab[:], in_=W1[:, D - 15 : D + 1].rearrange("(q t) k -> q t k", t=TILES))
+        b1raw = const.tile([P, TILES], BF16, name="b1raw", tag="b1raw")
+        nc.sync.dma_start(out=b1raw[:], in_=b1.rearrange("(q t) -> q t", t=TILES))
+        w1a = const.tile([P, TILES, D], BF16, name="w1a", tag="w1a")
+        nc.sync.dma_start(out=w1a[:], in_=W1[:, 0:D].rearrange("(q t) k -> q t k", t=TILES))
+        w2raw = const.tile([P, MID], BF16, name="w2raw", tag="w2raw")
+        nc.sync.dma_start(out=w2raw[:], in_=W2)
+        load(0, 2)
+        b2raw = const.tile([P, 1], BF16, name="b2raw", tag="b2raw")
+        nc.sync.dma_start(out=b2raw[:], in_=b2.rearrange("(o x) -> o x", x=1))
+        load(1, 1)
+
+        wl32 = const.tile([P, TILES, 1], F32, name="wl32", tag="wl32")
+        nc.vector.tensor_copy(out=wl32[:], in_=wslab[:, :, 15:16])
+        b132 = const.tile([P, TILES], F32, name="b132", tag="b132")
+        nc.vector.tensor_copy(out=b132[:], in_=b1raw[:])
+
+        def turn(words, first_tile, n_tiles):
+            xt = psum.tile([P, 2, 2, P], F32, name="xt", tag="xt", bufs=2)
+            for a in range(n_tiles):
+                base = (first_tile + a) * (D // 2)
+                for u in range(2):
+                    nc.tensor.transpose(xt[:, a, u, :], words[:, base + u : base + D // 2 : 2], ident_f[:])
+            return xt
+
+        def lay(xt, grouped, first_tile, n_tiles):
+            gw = grouped[:].bitcast(F32).rearrange("p (a e u) -> p a e u", e=P, u=2)
+            nc.scalar.copy(
+                out=gw[:, first_tile : first_tile + n_tiles, :, :],
+                in_=xt[:, 0:n_tiles, :, :].rearrange("p a u e -> p a e u"),
+            )
+
+        def st_turn(g):
+            ch, h = divmod(g, 2)
+            words = xs_of[ch][:].rearrange("p j k -> p (j k)").bitcast(F32)
+            xt_of[g] = [turn(words, TILES * h + 2 * a2, 2) for a2 in range(2)]
+
+        def st_lay(g):
+            xg = work.tile([P, GROUP * 4], BF16, name="xg", tag="xg", bufs=2, align_bytes=64)
+            xg_of[g] = xg
+            for a2 in range(2):
+                lay(xt_of[g][a2], xg, 2 * a2, 2)
+
+        def st_qx(g):
+            xc = work.tile([P, GROUP], U32, name="xc", tag="xc", bufs=3, align_bytes=64)
+            xsc = work.tile([P, GROUP], U8, name="xsc", tag="xsc", bufs=3, align_bytes=64)
+            xq_of[g] = (xc, xsc)
+            nc.vector.quantize_mx(out=xc[:].bitcast(FP8X4), scales=xsc[:], in_=xg_of[g][:])
+
+        def st_ef(g):
+            ch, h = divmod(g, 2)
+            efp = psum.tile([P, TILES, P], F32, name="efp", tag="efp", bufs=1)
+            ef_of[g] = efp
+            nc.tensor.matmul(
+                out=efp[:],
+                lhsT=ident_b[:, ch : ch + 1].to_broadcast([P, P]),
+                rhs=ef4[:].rearrange("k (n j) -> k j n", j=CHUNK_TILES)[:, TILES * h : TILES * (h + 1), :],
+                start=True,
+                stop=True,
+            )
+
+        def st_c(g):
+            c = work.tile([P, TILES, GROUP], F32, name="c", tag="c", bufs=2)
+            c_of[g] = c
+            for t in range(TILES):
+                nc.scalar.activation(
+                    out=c[:, t, :],
+                    in_=ef_of[g][:].rearrange("p j n -> p (j n)"),
+                    func=ACT.Identity,
+                    bias=b132[:, t : t + 1],
+                    scale=wl32[:, t, :],
+                )
+
+        def st_m1(g, j):
+            s1 = psum.tile([P, TILES, P], BANK_DT, name="s1", tag="s1", bufs=3)
+            s1_of[(g, j)] = s1
+            xc, xsc = xq_of[g]
+            cols = slice(j * P, (j + 1) * P)
+            for t in range(TILES):
+                wcols = slice(t * P, (t + 1) * P)
+                nc.tensor.matmul_mx(
+                    out=s1[:, t, :],
+                    lhsT=w1c[:, wcols].bitcast(FP8X4),
+                    lhsT_scale=w1s[:, wcols],
+                    rhs=xc[:, cols].bitcast(FP8X4),
+                    rhs_scale=xsc[:, cols],
+                    start=True,
+                    stop=True,
+                )
+
+        def st_b2(g, j):
+            if j == 0:
+                hp_new = work.tile([P, TILES, P, 4], BF16, name="hp", tag="hp", bufs=2)
+                hp_of[g] = hp_new
+            nc.vector.tensor_tensor(
+                out=hp_of[g][:, j, :, :],
+                in0=s1_of[(g, j)][:].rearrange("p t n -> p n t"),
+                in1=c_of[g][:, :, j * P : (j + 1) * P].rearrange("p t n -> p n t"),
+                op=ALU.add,
+            )
+
+        def st_relu(g):
+            hq = work.tile([P, GROUP * 4], BF16, name="hq", tag="hq", bufs=2, align_bytes=64)
+            hq_of[g] = hq
+            nc.vector.tensor_scalar_max(out=hq[:], in0=hp_of[g][:].rearrange("p j n t -> p (j n t)"), scalar1=0.0)
+
+        def st_qh(g):
+            hc = work.tile([P, GROUP], U32, name="hc", tag="hc", bufs=2, align_bytes=64)
+            hsc = work.tile([P, GROUP], U8, name="hsc", tag="hsc", bufs=2, align_bytes=64)
+            hc_of[g] = (hc, hsc)
+            nc.vector.quantize_mx(out=hc[:].bitcast(FP8X4), scales=hsc[:], in_=hq_of[g][:])
+
+        def st_m2(g):
+            s2 = psum.tile([P, GROUP], F32, name="s2", tag="s2", bufs=1)
+            s2_of[g] = s2
+            hc, hsc = hc_of[g]
+            nc.tensor.matmul_mx(
+                out=s2[:],
+                lhsT=w2c[:].bitcast(FP8X4),
+                lhsT_scale=w2s[:],
+                rhs=hc[:].bitcast(FP8X4),
+                rhs_scale=hsc[:],
+                start=True,
+                stop=True,
+            )
+
+        def st_tanh(g):
+            yt = work.tile([P, GROUP], F32, name="yt", tag="yt", bufs=2)
+            yt_of[g] = yt
+            nc.scalar.activation(out=yt[:], in_=s2_of[g][:], func=ACT.Tanh, bias=b2c32[:, 0:1])
+
+        def st_back(g):
+            s3 = psum.tile([P, TILES, OUT], F32, name="s3", tag="s3", bufs=1)
+            s3_of[g] = s3
+            for j in range(TILES):
+                nc.tensor.transpose(s3[:, j, :], yt_of[g][:, j * P : (j + 1) * P], ident_f[:])
+
+        def on_vector(g):
+            return g % 2 == 1
+
+        def st_out(g):
+            y = work.tile([P, TILES, OUT], F32, name="y", tag="y", bufs=3)
+            y_of[g] = y
+            if on_vector(g):
+                nc.vector.tensor_copy(out=y[:], in_=s3_of[g][:])
+            else:
+                nc.scalar.copy(out=y[:], in_=s3_of[g][:])
+            ch, h = divmod(g, 2)
+            rows = slice(ch * CHUNK, (ch + 1) * CHUNK)
+            nc.sync.dma_start(
+                out=out[rows, :].rearrange("(p j) o -> p j o", j=CHUNK_TILES)[:, TILES * h : TILES * (h + 1), :],
+                in_=y[:],
+            )
+
+        st_ef(0)
+        st_c(0)
+
+        w1words = w1a[:].rearrange("p t k -> p (t k)").bitcast(F32)
+        w1g = const.tile([P, TILES * P * 4], BF16, name="w1g", tag="w1g", align_bytes=64)
+        w1c = const.tile([P, MID], U32, name="w1c", tag="w1c", align_bytes=64)
+        w1s = const.tile([P, MID], U8, name="w1s", tag="w1s", align_bytes=64)
+        for half in range(2):
+            wt = turn(w1words, 2 * half, 2)
+            lay(wt, w1g, 2 * half, 2)
+        nc.vector.quantize_mx(out=w1c[:].bitcast(FP8X4), scales=w1s[:], in_=w1g[:])
+
+        w2g = const.tile([P, P * 4], BF16, name="w2g", tag="w2g", align_bytes=64)
+        w2c = const.tile([P, OUT], U32, name="w2c", tag="w2c", align_bytes=64)
+        w2s = const.tile([P, OUT], U8, name="w2s", tag="w2s", align_bytes=64)
+        wt2 = turn(w2raw[:].bitcast(F32), 0, 1)
+        lay(wt2, w2g, 0, 1)
+        nc.vector.quantize_mx(out=w2c[:].bitcast(FP8X4), scales=w2s[:], in_=w2g[:])
+        st_ef(1)
+        b2c32 = const.tile([P, 1], F32, name="b2c32", tag="b2c32")
+
+        def live(g):
+            return 0 <= g < NG
+
+        for s in range(-3, NG + 2):
+            late = s < 1
+            if (s + 7) % 2 == 0 and 2 <= (s + 7) // 2 < NCH:
+                load((s + 7) // 2, 1)
+            if live(s - 2):
+                st_back(s - 2)
+            if live(s + 3) and not late:
+                st_turn(s + 3)
+            if live(s + 1) and s + 1 >= 2:
+                st_c(s + 1)
+            if live(s):
+                st_b2(s, 0)
+                st_m1(s, 3)
+                st_b2(s, 1)
+            if live(s + 1):
+                st_m1(s + 1, 0)
+            if live(s - 2) and on_vector(s - 2):
+                st_out(s - 2)
+            if live(s - 1):
+                st_qh(s - 1)
+                st_m2(s - 1)
+            if live(s + 2) and s + 2 >= 2:
+                st_ef(s + 2)
+            if live(s + 3) and not late:
+                st_lay(s + 3)
+            if live(s - 1):
+                st_tanh(s - 1)
+            if live(s - 2) and not on_vector(s - 2):
+                st_out(s - 2)
+            if live(s):
+                st_b2(s, 2)
+            if live(s + 1):
+                st_m1(s + 1, 1)
+            if live(s):
+                st_b2(s, 3)
+            if live(s + 1):
+                st_m1(s + 1, 2)
+            if live(s + 2):
+                st_qx(s + 2)
+            if live(s):
+                st_relu(s)
+            if live(s + 3) and late:
+                st_turn(s + 3)
+                st_lay(s + 3)
+            if s == -2:
+                st_c(1)
+                nc.vector.tensor_copy(out=b2c32[:], in_=b2raw[:])

@@ -179,9 +179,9 @@ def tile_edgenetwork_kernel(
                 hp_new = work.tile([P, TILES, P, 4], BF16, name="hp", tag="hp", bufs=2)
                 hp_of[g] = hp_new
             nc.vector.tensor_tensor(
-                out=hp_of[g][:, j, :, :],
-                in0=s1_of[(g, j)][:].rearrange("p t n -> p n t"),
-                in1=c_of[g][:, :, j * P : (j + 1) * P].rearrange("p t n -> p n t"),
+                out=hp_of[g][:, j, :, :].rearrange("p (b i) t -> p b t i", i=4),
+                in0=s1_of[(g, j)][:].rearrange("p t (b i) -> p b t i", i=4),
+                in1=c_of[g][:, :, j * P : (j + 1) * P].rearrange("p t (b i) -> p b t i", i=4),
                 op=ALU.add,
             )
 

@@ -26,10 +26,21 @@ NG = E // GROUP
 NCH = E // CHUNK
 
 
+def unit_map(units):
+    table = {}
+    for g0, n in units:
+        for g in range(g0, g0 + n):
+            table[g] = (g0, n)
+    return table
+
+
 def tile_edgenetwork_kernel(
     tc, dst_node_feat, dst_node_hidden, src_node_feat, src_node_hidden, edge_feat, W1, b1, W2, b2, out
 ):
     nc = tc.nc
+    c_split = unit_map([(0, 1), (1, 1)] + [(g, 2) for g in range(2, NG, 2)])
+    x_split = unit_map([(g, 1) for g in range(NG)])
+    last_split = unit_map([(g, 1) for g in range(NG)])
     parts = (
         (dst_node_feat, 0, F),
         (dst_node_hidden, F, H),
@@ -56,7 +67,6 @@ def tile_edgenetwork_kernel(
         s2_of = {}
         yt_of = {}
         s3_of = {}
-        y_of = {}
 
         def load(ch, pieces):
             xs = work.tile([P, CHUNK_TILES, D], BF16, name="xs", tag="xs", bufs=3)
@@ -109,12 +119,14 @@ def tile_edgenetwork_kernel(
                     nc.tensor.transpose(xt[:, a, u, :], words[:, base + u : base + D // 2 : 2], ident_f[:])
             return xt
 
-        def lay(xt, grouped, first_tile, n_tiles):
+        def lay(xt, grouped, first_tile, n_tiles, by_vector):
             gw = grouped[:].bitcast(F32).rearrange("p (a e u) -> p a e u", e=P, u=2)
-            nc.scalar.copy(
-                out=gw[:, first_tile : first_tile + n_tiles, :, :],
-                in_=xt[:, 0:n_tiles, :, :].rearrange("p a u e -> p a e u"),
-            )
+            dst = gw[:, first_tile : first_tile + n_tiles, :, :]
+            src = xt[:, 0:n_tiles, :, :].rearrange("p a u e -> p a e u")
+            if by_vector:
+                nc.vector.tensor_copy(out=dst, in_=src)
+            else:
+                nc.scalar.copy(out=dst, in_=src)
 
         def st_turn(g):
             ch, h = divmod(g, 2)
@@ -122,46 +134,54 @@ def tile_edgenetwork_kernel(
             xt_of[g] = [turn(words, TILES * h + 2 * a2, 2) for a2 in range(2)]
 
         def st_lay(g):
-            xg = work.tile([P, GROUP * 4], BF16, name="xg", tag="xg", bufs=2, align_bytes=64)
-            xg_of[g] = xg
+            g0, n = x_split[g]
+            if g == g0:
+                xg_new = work.tile([P, n * GROUP * 4], BF16, name="xg", tag="xg", bufs=2, align_bytes=64)
+                xg_of[g0] = xg_new
             for a2 in range(2):
-                lay(xt_of[g][a2], xg, 2 * a2, 2)
+                lay(xt_of[g][a2], xg_of[g0], TILES * (g - g0) + 2 * a2, 2, g == 0)
 
-        def st_qx(g):
-            xc = work.tile([P, GROUP], U32, name="xc", tag="xc", bufs=3, align_bytes=64)
-            xsc = work.tile([P, GROUP], U8, name="xsc", tag="xsc", bufs=3, align_bytes=64)
-            xq_of[g] = (xc, xsc)
-            nc.vector.quantize_mx(out=xc[:].bitcast(FP8X4), scales=xsc[:], in_=xg_of[g][:])
+        def st_qx(g0):
+            n = x_split[g0][1]
+            xc = work.tile([P, n * GROUP], U32, name="xc", tag="xc", bufs=3, align_bytes=64)
+            xsc = work.tile([P, n * GROUP], U8, name="xsc", tag="xsc", bufs=3, align_bytes=64)
+            xq_of[g0] = (xc, xsc)
+            nc.vector.quantize_mx(out=xc[:].bitcast(FP8X4), scales=xsc[:], in_=xg_of[g0][:])
 
-        def st_ef(g):
-            ch, h = divmod(g, 2)
-            efp = psum.tile([P, TILES, P], F32, name="efp", tag="efp", bufs=1)
-            ef_of[g] = efp
-            nc.tensor.matmul(
-                out=efp[:],
-                lhsT=ident_b[:, ch : ch + 1].to_broadcast([P, P]),
-                rhs=ef4[:].rearrange("k (n j) -> k j n", j=CHUNK_TILES)[:, TILES * h : TILES * (h + 1), :],
-                start=True,
-                stop=True,
-            )
-
-        def st_c(g):
-            c = work.tile([P, TILES, GROUP], F32, name="c", tag="c", bufs=2)
-            c_of[g] = c
-            for t in range(TILES):
-                nc.scalar.activation(
-                    out=c[:, t, :],
-                    in_=ef_of[g][:].rearrange("p j n -> p (j n)"),
-                    func=ACT.Identity,
-                    bias=b132[:, t : t + 1],
-                    scale=wl32[:, t, :],
+        def st_ef(g0):
+            n = c_split[g0][1]
+            efp = psum.tile([P, n * GROUP], BF16, name="efp", tag="efp", bufs=1)
+            ef_of[g0] = efp
+            for i in range(n):
+                ch, h = divmod(g0 + i, 2)
+                nc.tensor.matmul(
+                    out=efp[:, i * GROUP : (i + 1) * GROUP].rearrange("p (j n) -> p j n", j=TILES),
+                    lhsT=ident_b[:, ch : ch + 1].to_broadcast([P, P]),
+                    rhs=ef4[:].rearrange("k (n j) -> k j n", j=CHUNK_TILES)[:, TILES * h : TILES * (h + 1), :],
+                    start=True,
+                    stop=True,
                 )
+
+        def st_c(g0, t):
+            n = c_split[g0][1]
+            if t == 0:
+                c_new = work.tile([P, TILES, n * GROUP], F32, name="c", tag="c", bufs=3)
+                c_of[g0] = c_new
+            nc.scalar.activation(
+                out=c_of[g0][:, t, :],
+                in_=ef_of[g0][:],
+                func=ACT.Identity,
+                bias=b132[:, t : t + 1],
+                scale=wl32[:, t, :],
+            )
 
         def st_m1(g, j):
             s1 = psum.tile([P, TILES, P], BANK_DT, name="s1", tag="s1", bufs=3)
             s1_of[(g, j)] = s1
-            xc, xsc = xq_of[g]
-            cols = slice(j * P, (j + 1) * P)
+            g0 = x_split[g][0]
+            xc, xsc = xq_of[g0]
+            first = (TILES * (g - g0) + j) * P
+            cols = slice(first, first + P)
             for t in range(TILES):
                 wcols = slice(t * P, (t + 1) * P)
                 nc.tensor.matmul_mx(
@@ -175,37 +195,44 @@ def tile_edgenetwork_kernel(
                 )
 
         def st_b2(g, j):
-            if j == 0:
-                hp_new = work.tile([P, TILES, P, 4], BF16, name="hp", tag="hp", bufs=2)
-                hp_of[g] = hp_new
+            h0, hn = last_split[g]
+            if g == h0 and j == 0:
+                hp_new = work.tile([P, hn * TILES, P, 4], BF16, name="hp", tag="hp", bufs=2)
+                hp_of[h0] = hp_new
+            c0 = c_split[g][0]
+            first = (g - c0) * GROUP + j * P
             nc.vector.tensor_tensor(
-                out=hp_of[g][:, j, :, :].rearrange("p (b i) t -> p b t i", i=4),
+                out=hp_of[h0][:, TILES * (g - h0) + j, :, :].rearrange("p (b i) t -> p b t i", i=4),
                 in0=s1_of[(g, j)][:].rearrange("p t (b i) -> p b t i", i=4),
-                in1=c_of[g][:, :, j * P : (j + 1) * P].rearrange("p t (b i) -> p b t i", i=4),
+                in1=c_of[c0][:, :, first : first + P].rearrange("p t (b i) -> p b t i", i=4),
                 op=ALU.add,
             )
 
-        def st_relu(g):
-            hq = work.tile([P, GROUP * 4], BF16, name="hq", tag="hq", bufs=2, align_bytes=64)
-            hq_of[g] = hq
-            nc.vector.tensor_scalar_max(out=hq[:], in0=hp_of[g][:].rearrange("p j n t -> p (j n t)"), scalar1=0.0)
+        def st_relu(h0):
+            hn = last_split[h0][1]
+            hq = work.tile([P, hn * GROUP * 4], BF16, name="hq", tag="hq", bufs=2, align_bytes=64)
+            hq_of[h0] = hq
+            nc.vector.tensor_scalar_max(out=hq[:], in0=hp_of[h0][:].rearrange("p j n t -> p (j n t)"), scalar1=0.0)
 
-        def st_qh(g):
-            hc = work.tile([P, GROUP], U32, name="hc", tag="hc", bufs=2, align_bytes=64)
-            hsc = work.tile([P, GROUP], U8, name="hsc", tag="hsc", bufs=2, align_bytes=64)
-            hc_of[g] = (hc, hsc)
-            nc.vector.quantize_mx(out=hc[:].bitcast(FP8X4), scales=hsc[:], in_=hq_of[g][:])
+        def st_qh(h0):
+            hn = last_split[h0][1]
+            hc = work.tile([P, hn * GROUP], U32, name="hc", tag="hc", bufs=2, align_bytes=64)
+            hsc = work.tile([P, hn * GROUP], U8, name="hsc", tag="hsc", bufs=2, align_bytes=64)
+            hc_of[h0] = (hc, hsc)
+            nc.vector.quantize_mx(out=hc[:].bitcast(FP8X4), scales=hsc[:], in_=hq_of[h0][:])
 
         def st_m2(g):
             s2 = psum.tile([P, GROUP], F32, name="s2", tag="s2", bufs=1)
             s2_of[g] = s2
-            hc, hsc = hc_of[g]
+            h0 = last_split[g][0]
+            hc, hsc = hc_of[h0]
+            cols = slice((g - h0) * GROUP, (g - h0 + 1) * GROUP)
             nc.tensor.matmul_mx(
                 out=s2[:],
                 lhsT=w2c[:].bitcast(FP8X4),
                 lhsT_scale=w2s[:],
-                rhs=hc[:].bitcast(FP8X4),
-                rhs_scale=hsc[:],
+                rhs=hc[:, cols].bitcast(FP8X4),
+                rhs_scale=hsc[:, cols],
                 start=True,
                 stop=True,
             )
@@ -222,11 +249,10 @@ def tile_edgenetwork_kernel(
                 nc.tensor.transpose(s3[:, j, :], yt_of[g][:, j * P : (j + 1) * P], ident_f[:])
 
         def on_vector(g):
-            return g % 2 == 1
+            return g % 4 == 1
 
         def st_out(g):
             y = work.tile([P, TILES, OUT], F32, name="y", tag="y", bufs=3)
-            y_of[g] = y
             if on_vector(g):
                 nc.vector.tensor_copy(out=y[:], in_=s3_of[g][:])
             else:
@@ -239,7 +265,8 @@ def tile_edgenetwork_kernel(
             )
 
         st_ef(0)
-        st_c(0)
+        for t in range(TILES):
+            st_c(0, t)
 
         w1words = w1a[:].rearrange("p t k -> p (t k)").bitcast(F32)
         w1g = const.tile([P, TILES * P * 4], BF16, name="w1g", tag="w1g", align_bytes=64)
@@ -247,44 +274,47 @@ def tile_edgenetwork_kernel(
         w1s = const.tile([P, MID], U8, name="w1s", tag="w1s", align_bytes=64)
         for half in range(2):
             wt = turn(w1words, 2 * half, 2)
-            lay(wt, w1g, 2 * half, 2)
+            lay(wt, w1g, 2 * half, 2, True)
         nc.vector.quantize_mx(out=w1c[:].bitcast(FP8X4), scales=w1s[:], in_=w1g[:])
+
+        st_ef(1)
+        for t in range(TILES):
+            st_c(1, t)
 
         w2g = const.tile([P, P * 4], BF16, name="w2g", tag="w2g", align_bytes=64)
         w2c = const.tile([P, OUT], U32, name="w2c", tag="w2c", align_bytes=64)
         w2s = const.tile([P, OUT], U8, name="w2s", tag="w2s", align_bytes=64)
-        wt2 = turn(w2raw[:].bitcast(F32), 0, 1)
-        lay(wt2, w2g, 0, 1)
-        nc.vector.quantize_mx(out=w2c[:].bitcast(FP8X4), scales=w2s[:], in_=w2g[:])
-        st_ef(1)
         b2c32 = const.tile([P, 1], F32, name="b2c32", tag="b2c32")
 
         def live(g):
             return 0 <= g < NG
 
         for s in range(-3, NG + 2):
-            late = s < 1
+            late = s in (-1, 0)
             if (s + 7) % 2 == 0 and 2 <= (s + 7) // 2 < NCH:
                 load((s + 7) // 2, 1)
             if live(s - 2):
                 st_back(s - 2)
             if live(s + 3) and not late:
                 st_turn(s + 3)
-            if live(s + 1) and s + 1 >= 2:
-                st_c(s + 1)
+            if s >= 0 and live(s + 2 - s % 2):
+                for t in (2 * (s % 2), 2 * (s % 2) + 1):
+                    st_c(s + 2 - s % 2, t)
             if live(s):
                 st_b2(s, 0)
                 st_m1(s, 3)
                 st_b2(s, 1)
-            if live(s + 1):
+            if s == 0:
+                st_qx(1)
+            if live(s + 1) and s >= 0:
                 st_m1(s + 1, 0)
             if live(s - 2) and on_vector(s - 2):
                 st_out(s - 2)
             if live(s - 1):
                 st_qh(s - 1)
                 st_m2(s - 1)
-            if live(s + 2) and s + 2 >= 2:
-                st_ef(s + 2)
+            if s % 2 == 1 and s + 3 >= 2 and live(s + 3):
+                st_ef(s + 3)
             if live(s + 3) and not late:
                 st_lay(s + 3)
             if live(s - 1):
@@ -293,19 +323,25 @@ def tile_edgenetwork_kernel(
                 st_out(s - 2)
             if live(s):
                 st_b2(s, 2)
-            if live(s + 1):
+            if live(s + 1) and s >= 0:
                 st_m1(s + 1, 1)
             if live(s):
                 st_b2(s, 3)
-            if live(s + 1):
+            if live(s + 1) and s >= 0:
                 st_m1(s + 1, 2)
-            if live(s + 2):
+            if live(s + 2) and s + 2 != 1:
                 st_qx(s + 2)
+            if s == -2:
+                for j in range(3):
+                    st_m1(0, j)
             if live(s):
                 st_relu(s)
+            if s == 0:
+                nc.vector.quantize_mx(out=w2c[:].bitcast(FP8X4), scales=w2s[:], in_=w2g[:])
+                nc.vector.tensor_copy(out=b2c32[:], in_=b2raw[:])
             if live(s + 3) and late:
                 st_turn(s + 3)
                 st_lay(s + 3)
             if s == -2:
-                st_c(1)
-                nc.vector.tensor_copy(out=b2c32[:], in_=b2raw[:])
+                wt2 = turn(w2raw[:].bitcast(F32), 0, 1)
+                lay(wt2, w2g, 0, 1, False)

from contextlib import ExitStack

import concourse.mybir as mybir
from concourse.masks import make_identity

E, F, H, MID, OUT = 16384, 64, 192, 512, 128
D = 2 * (F + H)
FLOPS = 2 * E * MID * (D + 1) + 2 * E * MID * OUT

F32 = mybir.dt.float32
BF16 = mybir.dt.bfloat16
U32 = mybir.dt.uint32
U8 = mybir.dt.uint8
FP8X4 = mybir.dt.float8_e4m3fn_x4
ALU = mybir.AluOpType
ACT = mybir.ActivationFunctionType

BANK_DT = F32

P = 128
TILES = 4
GROUP = TILES * P
CHUNK_TILES = 8
CHUNK = CHUNK_TILES * P
NG = E // GROUP
NCH = E // CHUNK


def unit_map(units):
    table = {}
    for g0, n in units:
        for g in range(g0, g0 + n):
            table[g] = (g0, n)
    return table


def tile_edgenetwork_kernel(
    tc, dst_node_feat, dst_node_hidden, src_node_feat, src_node_hidden, edge_feat, W1, b1, W2, b2, out
):
    nc = tc.nc
    c_split = unit_map([(0, 1), (1, 1)] + [(g, 2) for g in range(2, NG, 2)])
    x_split = unit_map([(g, 1) for g in range(NG)])
    last_split = unit_map([(g, 1) for g in range(NG)])
    parts = (
        (dst_node_feat, 0, F),
        (dst_node_hidden, F, H),
        (src_node_feat, F + H, F),
        (src_node_hidden, 2 * F + H, H),
    )

    with ExitStack() as ctx:
        const = ctx.enter_context(tc.tile_pool(name="const", bufs=1))
        work = ctx.enter_context(tc.tile_pool(name="work", bufs=2))
        psum = ctx.enter_context(tc.psum_pool(name="psum", bufs=1))
        ctx.enter_context(tc.manual_schedule())

        xs_of = {}
        xt_of = {}
        xg_of = {}
        xq_of = {}
        ef_of = {}
        c_of = {}
        s1_of = {}
        hp_of = {}
        hq_of = {}
        hc_of = {}
        s2_of = {}
        yt_of = {}
        s3_of = {}

        def load(ch, pieces):
            xs = work.tile([P, CHUNK_TILES, D], BF16, name="xs", tag="xs", bufs=3)
            xs_of[ch] = xs
            rows = slice(ch * CHUNK, (ch + 1) * CHUNK)
            step = CHUNK_TILES // pieces
            for j0 in range(0, CHUNK_TILES, step):
                for src, k0, width in parts:
                    nc.sync.dma_start(
                        out=xs[:, j0 : j0 + step, k0 : k0 + width],
                        in_=src[rows, :].rearrange("(p j) k -> p j k", j=CHUNK_TILES)[:, j0 : j0 + step, :],
                    )

        warm = const.tile([P, 1], F32, name="warm", tag="warm")
        nc.vector.memset(warm[:], 0.0)
        warm2 = const.tile([P, 1], F32, name="warm2", tag="warm2")
        nc.scalar.activation(out=warm2[:], in_=warm[:], func=ACT.Tanh)

        ident_b = const.tile([P, P], BF16, name="ident_b", tag="ident_b")
        make_identity(nc, ident_b[:])
        ident_f = const.tile([P, P], F32, name="ident_f", tag="ident_f")
        make_identity(nc, ident_f[:])

        ef4 = const.tile([P, CHUNK], BF16, name="ef4", tag="ef4")
        nc.vector.memset(ef4[:], 0.0)
        nc.sync.dma_start(out=ef4[0:NCH, :], in_=edge_feat.rearrange("(c r) -> c r", r=CHUNK))
        wslab = const.tile([P, TILES, 16], BF16, name="wslab", tag="wslab")
        nc.sync.dma_start(out=wslab[:], in_=W1[:, D - 15 : D + 1].rearrange("(q t) k -> q t k", t=TILES))
        b1raw = const.tile([P, TILES], BF16, name="b1raw", tag="b1raw")
        nc.sync.dma_start(out=b1raw[:], in_=b1.rearrange("(q t) -> q t", t=TILES))
        w1a = const.tile([P, TILES, D], BF16, name="w1a", tag="w1a")
        nc.sync.dma_start(out=w1a[:], in_=W1[:, 0:D].rearrange("(q t) k -> q t k", t=TILES))
        w2raw = const.tile([P, MID], BF16, name="w2raw", tag="w2raw")
        nc.sync.dma_start(out=w2raw[:], in_=W2)
        load(0, 2)
        b2raw = const.tile([P, 1], BF16, name="b2raw", tag="b2raw")
        nc.sync.dma_start(out=b2raw[:], in_=b2.rearrange("(o x) -> o x", x=1))
        load(1, 1)

        wl32 = const.tile([P, TILES, 1], F32, name="wl32", tag="wl32")
        nc.vector.tensor_copy(out=wl32[:], in_=wslab[:, :, 15:16])
        b132 = const.tile([P, TILES], F32, name="b132", tag="b132")
        nc.vector.tensor_copy(out=b132[:], in_=b1raw[:])

        def turn(words, first_tile, n_tiles):
            xt = psum.tile([P, 2, 2, P], F32, name="xt", tag="xt", bufs=2)
            for a in range(n_tiles):
                base = (first_tile + a) * (D // 2)
                for u in range(2):
                    nc.tensor.transpose(xt[:, a, u, :], words[:, base + u : base + D // 2 : 2], ident_f[:])
            return xt

        def lay(xt, grouped, first_tile, n_tiles, by_vector):
            gw = grouped[:].bitcast(F32).rearrange("p (a e u) -> p a e u", e=P, u=2)
            dst = gw[:, first_tile : first_tile + n_tiles, :, :]
            src = xt[:, 0:n_tiles, :, :].rearrange("p a u e -> p a e u")
            if by_vector:
                nc.vector.tensor_copy(out=dst, in_=src)
            else:
                nc.scalar.copy(out=dst, in_=src)

        def st_turn(g):
            ch, h = divmod(g, 2)
            words = xs_of[ch][:].rearrange("p j k -> p (j k)").bitcast(F32)
            xt_of[g] = [turn(words, TILES * h + 2 * a2, 2) for a2 in range(2)]

        def st_lay(g):
            g0, n = x_split[g]
            if g == g0:
                xg_new = work.tile([P, n * GROUP * 4], BF16, name="xg", tag="xg", bufs=2, align_bytes=64)
                xg_of[g0] = xg_new
            for a2 in range(2):
                lay(xt_of[g][a2], xg_of[g0], TILES * (g - g0) + 2 * a2, 2, g == 0)

        def st_qx(g0):
            n = x_split[g0][1]
            xc = work.tile([P, n * GROUP], U32, name="xc", tag="xc", bufs=3, align_bytes=64)
            xsc = work.tile([P, n * GROUP], U8, name="xsc", tag="xsc", bufs=3, align_bytes=64)
            xq_of[g0] = (xc, xsc)
            nc.vector.quantize_mx(out=xc[:].bitcast(FP8X4), scales=xsc[:], in_=xg_of[g0][:])

        def st_ef(g0):
            n = c_split[g0][1]
            efp = psum.tile([P, n * GROUP], BF16, name="efp", tag="efp", bufs=1)
            ef_of[g0] = efp
            for i in range(n):
                ch, h = divmod(g0 + i, 2)
                nc.tensor.matmul(
                    out=efp[:, i * GROUP : (i + 1) * GROUP].rearrange("p (j n) -> p j n", j=TILES),
                    lhsT=ident_b[:, ch : ch + 1].to_broadcast([P, P]),
                    rhs=ef4[:].rearrange("k (n j) -> k j n", j=CHUNK_TILES)[:, TILES * h : TILES * (h + 1), :],
                    start=True,
                    stop=True,
                )

        def st_c(g0, t):
            n = c_split[g0][1]
            if t == 0:
                c_new = work.tile([P, TILES, n * GROUP], F32, name="c", tag="c", bufs=3)
                c_of[g0] = c_new
            nc.scalar.activation(
                out=c_of[g0][:, t, :],
                in_=ef_of[g0][:],
                func=ACT.Identity,
                bias=b132[:, t : t + 1],
                scale=wl32[:, t, :],
            )

        def st_m1(g, j):
            s1 = psum.tile([P, TILES, P], BANK_DT, name="s1", tag="s1", bufs=3)
            s1_of[(g, j)] = s1
            g0 = x_split[g][0]
            xc, xsc = xq_of[g0]
            first = (TILES * (g - g0) + j) * P
            cols = slice(first, first + P)
            for t in range(TILES):
                wcols = slice(t * P, (t + 1) * P)
                nc.tensor.matmul_mx(
                    out=s1[:, t, :],
                    lhsT=w1c[:, wcols].bitcast(FP8X4),
                    lhsT_scale=w1s[:, wcols],
                    rhs=xc[:, cols].bitcast(FP8X4),
                    rhs_scale=xsc[:, cols],
                    start=True,
                    stop=True,
                )

        def st_b2(g, j):
            h0, hn = last_split[g]
            if g == h0 and j == 0:
                hp_new = work.tile([P, hn * TILES, P, 4], BF16, name="hp", tag="hp", bufs=2)
                hp_of[h0] = hp_new
            c0 = c_split[g][0]
            first = (g - c0) * GROUP + j * P
            nc.vector.tensor_tensor(
                out=hp_of[h0][:, TILES * (g - h0) + j, :, :].rearrange("p (b i) t -> p b t i", i=4),
                in0=s1_of[(g, j)][:].rearrange("p t (b i) -> p b t i", i=4),
                in1=c_of[c0][:, :, first : first + P].rearrange("p t (b i) -> p b t i", i=4),
                op=ALU.add,
            )

        def st_relu(h0):
            hn = last_split[h0][1]
            hq = work.tile([P, hn * GROUP * 4], BF16, name="hq", tag="hq", bufs=2, align_bytes=64)
            hq_of[h0] = hq
            nc.vector.tensor_scalar_max(out=hq[:], in0=hp_of[h0][:].rearrange("p j n t -> p (j n t)"), scalar1=0.0)

        def st_qh(h0):
            hn = last_split[h0][1]
            hc = work.tile([P, hn * GROUP], U32, name="hc", tag="hc", bufs=2, align_bytes=64)
            hsc = work.tile([P, hn * GROUP], U8, name="hsc", tag="hsc", bufs=2, align_bytes=64)
            hc_of[h0] = (hc, hsc)
            nc.vector.quantize_mx(out=hc[:].bitcast(FP8X4), scales=hsc[:], in_=hq_of[h0][:])

        def st_m2(g):
            s2 = psum.tile([P, GROUP], F32, name="s2", tag="s2", bufs=1)
            s2_of[g] = s2
            h0 = last_split[g][0]
            hc, hsc = hc_of[h0]
            cols = slice((g - h0) * GROUP, (g - h0 + 1) * GROUP)
            nc.tensor.matmul_mx(
                out=s2[:],
                lhsT=w2c[:].bitcast(FP8X4),
                lhsT_scale=w2s[:],
                rhs=hc[:, cols].bitcast(FP8X4),
                rhs_scale=hsc[:, cols],
                start=True,
                stop=True,
            )

        def st_tanh(g):
            yt = work.tile([P, GROUP], F32, name="yt", tag="yt", bufs=2)
            yt_of[g] = yt
            nc.scalar.activation(out=yt[:], in_=s2_of[g][:], func=ACT.Tanh, bias=b2c32[:, 0:1])

        def st_back(g):
            s3 = psum.tile([P, TILES, OUT], F32, name="s3", tag="s3", bufs=1)
            s3_of[g] = s3
            for j in range(TILES):
                nc.tensor.transpose(s3[:, j, :], yt_of[g][:, j * P : (j + 1) * P], ident_f[:])

        def on_vector(g):
            return g % 4 == 1

        def st_out(g):
            y = work.tile([P, TILES, OUT], F32, name="y", tag="y", bufs=3)
            if on_vector(g):
                nc.vector.tensor_copy(out=y[:], in_=s3_of[g][:])
            else:
                nc.scalar.copy(out=y[:], in_=s3_of[g][:])
            ch, h = divmod(g, 2)
            rows = slice(ch * CHUNK, (ch + 1) * CHUNK)
            nc.sync.dma_start(
                out=out[rows, :].rearrange("(p j) o -> p j o", j=CHUNK_TILES)[:, TILES * h : TILES * (h + 1), :],
                in_=y[:],
            )

        st_ef(0)
        for t in range(TILES):
            st_c(0, t)

        w1words = w1a[:].rearrange("p t k -> p (t k)").bitcast(F32)
        w1g = const.tile([P, TILES * P * 4], BF16, name="w1g", tag="w1g", align_bytes=64)
        w1c = const.tile([P, MID], U32, name="w1c", tag="w1c", align_bytes=64)
        w1s = const.tile([P, MID], U8, name="w1s", tag="w1s", align_bytes=64)
        for half in range(2):
            wt = turn(w1words, 2 * half, 2)
            lay(wt, w1g, 2 * half, 2, True)
        nc.vector.quantize_mx(out=w1c[:].bitcast(FP8X4), scales=w1s[:], in_=w1g[:])

        st_ef(1)
        for t in range(TILES):
            st_c(1, t)

        w2g = const.tile([P, P * 4], BF16, name="w2g", tag="w2g", align_bytes=64)
        w2c = const.tile([P, OUT], U32, name="w2c", tag="w2c", align_bytes=64)
        w2s = const.tile([P, OUT], U8, name="w2s", tag="w2s", align_bytes=64)
        b2c32 = const.tile([P, 1], F32, name="b2c32", tag="b2c32")

        def live(g):
            return 0 <= g < NG

        for s in range(-3, NG + 2):
            late = s in (-1, 0)
            if (s + 7) % 2 == 0 and 2 <= (s + 7) // 2 < NCH:
                load((s + 7) // 2, 1)
            if live(s - 2):
                st_back(s - 2)
            if live(s + 3) and not late:
                st_turn(s + 3)
            if s >= 0 and live(s + 2 - s % 2):
                for t in (2 * (s % 2), 2 * (s % 2) + 1):
                    st_c(s + 2 - s % 2, t)
            if live(s):
                st_b2(s, 0)
                st_m1(s, 3)
                st_b2(s, 1)
            if s == 0:
                st_qx(1)
            if live(s + 1) and s >= 0:
                st_m1(s + 1, 0)
            if live(s - 2) and on_vector(s - 2):
                st_out(s - 2)
            if live(s - 1):
                st_qh(s - 1)
                st_m2(s - 1)
            if s % 2 == 1 and s + 3 >= 2 and live(s + 3):
                st_ef(s + 3)
            if live(s + 3) and not late:
                st_lay(s + 3)
            if live(s - 1):
                st_tanh(s - 1)
            if live(s - 2) and not on_vector(s - 2):
                st_out(s - 2)
            if live(s):
                st_b2(s, 2)
            if live(s + 1) and s >= 0:
                st_m1(s + 1, 1)
            if live(s):
                st_b2(s, 3)
            if live(s + 1) and s >= 0:
                st_m1(s + 1, 2)
            if live(s + 2) and s + 2 != 1:
                st_qx(s + 2)
            if s == -2:
                for j in range(3):
                    st_m1(0, j)
            if live(s):
                st_relu(s)
            if s == 0:
                nc.vector.quantize_mx(out=w2c[:].bitcast(FP8X4), scales=w2s[:], in_=w2g[:])
                nc.vector.tensor_copy(out=b2c32[:], in_=b2raw[:])
            if live(s + 3) and late:
                st_turn(s + 3)
                st_lay(s + 3)
            if s == -2:
                wt2 = turn(w2raw[:].bitcast(F32), 0, 1)
                lay(wt2, w2g, 0, 1, False)
